import numpy as np
import ml_dtypes


def mxq(x, axis, fmt="e4m3"):
    dtype, down = {"e4m3": (ml_dtypes.float8_e4m3fn, 7), "e5m2": (ml_dtypes.float8_e5m2, 14)}[fmt]
    v = np.moveaxis(np.asarray(x, np.float32).astype(ml_dtypes.bfloat16).astype(np.float64), axis, -1)
    blocks = v.reshape(v.shape[:-1] + (-1, 32))
    amax = np.abs(blocks).max(-1, keepdims=True)
    byte = np.maximum(np.where(amax > 0, np.frexp(amax)[1] - 1 + 127, 0) - down, 1)
    scale = np.exp2(byte - 127.0)
    codes = (blocks / scale).astype(np.float32).astype(dtype).astype(np.float64)
    return np.moveaxis((codes * scale).reshape(v.shape), -1, axis)


WIDE = False


def mx_kscale(k):
    if not WIDE:
        return np.ones(k)
    levels = np.array([10, -10, 5, -5, 0])
    if k % 512:
        return np.exp2(np.random.permutation(np.resize(levels, k // 32))).repeat(32)
    a = np.empty((k // 512, 16))
    for p in range(k // 512):
        a[p, :8] = np.random.permutation(np.resize(levels, 8))
        for g in range(8):
            far = levels[np.abs(levels - a[p, g]) >= 10]
            a[p, g + 8] = far[np.random.randint(len(far))]
    return np.exp2(a.ravel()).repeat(32)


BF16 = ml_dtypes.bfloat16


def bf(x):
    return np.asarray(x, np.float32).astype(BF16)


def f64(x):
    return np.asarray(x).astype(np.float64)


B, RES, C, NH, RD, RW = 4, 32, 512, 8, 16, 128
N, L = B * RES, RES


def setup_inputs():
    s, t = mx_kscale(C), mx_kscale(C)
    return {"y_h": bf(np.random.standard_normal((N, L, C)) * 0.5 * s),
            "y_w": bf(np.random.standard_normal((N, L, C)) * 0.5 * s),
            "x": bf(np.random.standard_normal((B, RES, RES, C)) * s),
            "a_logits": bf(np.random.standard_normal((B, 3 * C))),
            "Wo_h": bf(np.random.standard_normal((C, C)) * 2.0 / np.sqrt(C) * t[:, None] / s),
            "bo_h": bf(np.random.standard_normal(C) * 0.3 * t),
            "Wo_w": bf(np.random.standard_normal((C, C)) * 2.0 / np.sqrt(C) * t[:, None] / s),
            "bo_w": bf(np.random.standard_normal(C) * 0.3 * t),
            "Wmlpc": bf(np.random.standard_normal((C, C)) / np.sqrt(C) * t[:, None] / s),
            "Wp": bf(np.random.standard_normal((C, C)) * 1.5 / np.sqrt(C) / t),
            "bp": bf(np.random.standard_normal(C) * 0.3)}


def reference(y_h, y_w, x, a_logits, Wo_h, bo_h, Wo_w, bo_w, Wmlpc, Wp, bp):
    h = (mxq(f64(y_h), 2, "e4m3") @ mxq(f64(Wo_h), 1, "e4m3").T) + f64(bo_h)
    h = h.reshape(B, RES, RES, C).transpose(0, 2, 1, 3)
    w = (mxq(f64(y_w), 2, "e4m3") @ mxq(f64(Wo_w), 1, "e4m3").T) + f64(bo_w)
    w = w.reshape(B, RES, RES, C)
    c = mxq(f64(x), 3, "e4m3") @ mxq(f64(Wmlpc), 1, "e4m3").T
    a = f64(a_logits).reshape(B, C, 3).transpose(2, 0, 1)
    a = np.exp(a - a.max(0, keepdims=True))
    a = (a / a.sum(0, keepdims=True))[:, :, None, None, :]
    out = h * a[0] + w * a[1] + c * a[2]
    return (mxq(out, 3, "e4m3") @ mxq(f64(Wp), 1, "e4m3").T) + f64(bp)

@@ -1,0 +1,261 @@
+from contextlib import ExitStack
+
+import concourse.mybir as mybir
+from concourse.masks import make_identity
+
+F32 = mybir.dt.float32
+BF16 = mybir.dt.bfloat16
+U32 = mybir.dt.uint32
+U8 = mybir.dt.uint8
+FP8X4 = mybir.dt.float8_e4m3fn_x4
+ALU = mybir.AluOpType
+ACT = mybir.ActivationFunctionType
+AXIS = mybir.AxisListType
+
+P = 128
+PACK = 4
+C = P * PACK
+IMAGES = 4
+RES = 32
+SLOTS = RES * RES // P
+TILE_SLOTS = 4
+TILE_PIXELS = TILE_SLOTS * P
+TILES = IMAGES * SLOTS // TILE_SLOTS
+BRANCHES = ("h", "w", "c")
+RAW_BUFS = 4
+STORE_SLOTS = 1
+GPSIMD_PIXELS = 224
+
+FLOPS = 4 * 2 * IMAGES * RES * RES * C * C
+
+NEIGHBOURS = "p (s q u) -> p s u q"
+
+
+def tile_dynamixerblock_pb_kernel(
+    tc, y_h, y_w, x, a_logits, Wo_h, bo_h, Wo_w, bo_w, Wmlpc, Wp, bp, out
+):
+    nc = tc.nc
+    ctx = ExitStack()
+    with ctx:
+        consts = ctx.enter_context(tc.tile_pool(name="consts", bufs=1))
+        raw_pool = ctx.enter_context(tc.tile_pool(name="raw", bufs=RAW_BUFS))
+        grouped_pool = ctx.enter_context(tc.tile_pool(name="grouped", bufs=4))
+        token_pool = ctx.enter_context(tc.tile_pool(name="tokens", bufs=2))
+        blend_pool = ctx.enter_context(tc.tile_pool(name="blend", bufs=2))
+        out_pool = ctx.enter_context(tc.tile_pool(name="results", bufs=6))
+        psum = ctx.enter_context(tc.psum_pool(name="psum", bufs=8))
+        ctx.enter_context(tc.manual_schedule())
+
+        def load_tokens(n, branch):
+            image, half = divmod(n, SLOTS // TILE_SLOTS)
+            first = half * TILE_SLOTS
+            raw = raw_pool.tile([P, TILE_SLOTS * C], BF16, tag="raw_" + branch, name="raw_" + branch)
+            if branch == "h":
+                for q in range(RES // SLOTS):
+                    columns = y_h[image * RES + q * SLOTS + first : image * RES + q * SLOTS + first + TILE_SLOTS]
+                    nc.sync.dma_start(
+                        out=raw[q : P : RES // SLOTS, :].rearrange("i (s k) -> i s k", s=TILE_SLOTS),
+                        in_=columns.rearrange("s i k -> i s k"),
+                    )
+            else:
+                rows = y_w[image * RES : (image + 1) * RES] if branch == "w" else x[image]
+                nc.sync.dma_start(
+                    out=raw[:].rearrange("p (s k) -> p s k", s=TILE_SLOTS),
+                    in_=rows.rearrange("i (q s) k -> (i q) s k", s=SLOTS)[:, first : first + TILE_SLOTS, :],
+                )
+            return raw
+
+        def load_weight(rows, name):
+            raw = raw_pool.tile([P, PACK * C], BF16, tag="raw_weight", name="raw_" + name)
+            nc.sync.dma_start(out=raw[:].rearrange("p (s k) -> p s k", s=PACK), in_=rows)
+            return raw
+
+        def turn(raw, word_order, vector_helps):
+            words = raw[:].bitcast(F32).rearrange(word_order, s=4, u=2)
+            grouped = grouped_pool.tile([P, 4 * P * PACK], BF16, tag="grouped", name="grouped", align_bytes=64)
+            pairs = grouped[:].bitcast(F32).rearrange("p (c u) -> p c u", u=2)
+            for half in range(2):
+                bank = psum.tile([P, 2, 2 * P], F32, tag="bank", name="turned")
+                for s in range(2):
+                    for u in range(2):
+                        nc.tensor.transpose(bank[:, u, s * P : (s + 1) * P], words[:, 2 * half + s, u, :], ident[:])
+                target = pairs[:, half * 2 * P : (half + 1) * 2 * P, :]
+                source = bank[:].rearrange("p u c -> p c u")
+                if vector_helps and half == 1:
+                    nc.vector.tensor_copy(out=target, in_=source)
+                else:
+                    nc.scalar.copy(out=target, in_=source)
+            return grouped
+
+        def quantise(grouped, pool, name):
+            codes = pool.tile([P, 4 * P], U32, tag="codes_" + name, name="codes_" + name, align_bytes=64)
+            scales = pool.tile([P, 4 * P], U8, tag="scales_" + name, name="scales_" + name, align_bytes=64)
+            nc.vector.quantize_mx(out=codes[:].bitcast(FP8X4), scales=scales[:], in_=grouped[:])
+            return codes, scales
+
+        def turn_tokens(n, branch, vector_helps):
+            if n < TILES:
+                turned_tokens[(n, branch)] = turn(raw_tokens[(n, branch)], NEIGHBOURS, vector_helps)
+                if n + RAW_BUFS < TILES:
+                    raw_tokens[(n + RAW_BUFS, branch)] = load_tokens(n + RAW_BUFS, branch)
+
+        def quantise_tokens(n, branch):
+            if n < TILES:
+                token_codes[(n, branch)] = quantise(turned_tokens[(n, branch)], token_pool, branch)
+
+        def project(n, t):
+            column = (n * TILE_SLOTS // SLOTS) * PACK + t
+            channels = slice(t * P, (t + 1) * P)
+            acc = {}
+            for branch in BRANCHES:
+                codes, scales = token_codes[(n, branch)]
+                acc[branch] = psum.tile([P, TILE_PIXELS], F32, tag="bank", name="acc_" + branch)
+                nc.tensor.matmul_mx(
+                    out=acc[branch][:],
+                    lhsT=weights[branch][0][:, channels].bitcast(FP8X4),
+                    lhsT_scale=weights[branch][1][:, channels],
+                    rhs=codes[:].bitcast(FP8X4),
+                    rhs_scale=scales[:],
+                    start=True,
+                    stop=True,
+                )
+            part_h = blend_pool.tile([P, TILE_PIXELS], F32, tag="part_h", name="part_h", bufs=3)
+            nc.scalar.activation(
+                out=part_h[:], in_=acc["h"][:], func=ACT.Identity,
+                scale=gate[:, column, 0:1], bias=shift[:, column : column + 1],
+            )
+            nc.scalar.activation(
+                out=part_w[n][:, t, :], in_=acc["w"][:], func=ACT.Copy, scale=gate[:, column, 1:2]
+            )
+            nc.vector.scalar_tensor_tensor(
+                out=part_hc[n][:, t, :], in0=acc["c"][:], scalar=gate[:, column, 2:3], in1=part_h[:],
+                op0=ALU.mult, op1=ALU.add,
+            )
+
+        def add_parts(engine, n, first, last):
+            runs = slice(first // 4, last // 4)
+            engine.tensor_tensor(
+                out=fused[n][:].rearrange("p (c i t) -> p c t i", i=4, t=PACK)[:, runs, :, :],
+                in0=part_hc[n][:].rearrange("p t (c i) -> p c t i", i=4)[:, runs, :, :],
+                in1=part_w[n][:].rearrange("p t (c i) -> p c t i", i=4)[:, runs, :, :],
+                op=ALU.add,
+            )
+
+        def output(n):
+            image, half = divmod(n, SLOTS // TILE_SLOTS)
+            codes, scales = fused_codes[n]
+            for first in range(0, TILE_SLOTS, STORE_SLOTS):
+                result = out_pool.tile([P, STORE_SLOTS, C], F32, tag="result", name="result")
+                for s in range(STORE_SLOTS):
+                    pixels = slice((first + s) * P, (first + s + 1) * P)
+                    acc = psum.tile([P, C], F32, tag="bank", name="acc_out")
+                    nc.tensor.matmul_mx(
+                        out=acc[:],
+                        lhsT=codes[:, pixels].bitcast(FP8X4),
+                        lhsT_scale=scales[:, pixels],
+                        rhs=weights["p"][0][:].bitcast(FP8X4),
+                        rhs_scale=weights["p"][1][:],
+                        start=True,
+                        stop=True,
+                    )
+                    nc.vector.tensor_tensor(out=result[:, s, :], in0=acc[:], in1=bp_all[:], op=ALU.add)
+                slot = half * TILE_SLOTS + first
+                nc.sync.dma_start(
+                    out=out[image].rearrange("i (q s) e -> (i q) s e", s=SLOTS)[:, slot : slot + STORE_SLOTS, :],
+                    in_=result[:],
+                )
+
+        ident = consts.tile([P, P], F32, name="ident")
+        make_identity(nc, ident[:])
+
+        logits_bf = consts.tile([P, IMAGES, PACK * 3], BF16, name="logits_bf")
+        nc.scalar.dma_start(out=logits_bf[:], in_=a_logits.rearrange("b (p c) -> p b c", c=PACK * 3))
+        bias_h = consts.tile([P, PACK], BF16, name="bias_h")
+        nc.scalar.dma_start(out=bias_h[:], in_=bo_h.rearrange("(p t) -> p t", t=PACK))
+        bias_w = consts.tile([P, PACK], BF16, name="bias_w")
+        nc.scalar.dma_start(out=bias_w[:], in_=bo_w.rearrange("(p t) -> p t", t=PACK))
+
+        raw_tokens = {}
+        raw_weights = {}
+        branch_weights = {"h": Wo_h, "w": Wo_w, "c": Wmlpc}
+        for branch in BRANCHES:
+            raw_weights[branch] = load_weight(
+                branch_weights[branch].rearrange("(p t) k -> p t k", t=PACK), branch
+            )
+            raw_tokens[(0, branch)] = load_tokens(0, branch)
+        for branch in BRANCHES:
+            raw_tokens[(1, branch)] = load_tokens(1, branch)
+        raw_weights["p"] = load_weight(Wp.rearrange("(s p) d -> p s d", p=P), "p")
+        bp_all = consts.tile([P, C], BF16, name="bp_all")
+        nc.sync.dma_start(out=bp_all[:], in_=bp.partition_broadcast(P))
+        for n in range(2, RAW_BUFS):
+            for branch in BRANCHES:
+                raw_tokens[(n, branch)] = load_tokens(n, branch)
+
+        groups = IMAGES * PACK
+        logits = consts.tile([P, groups, 3], F32, name="logits")
+        nc.vector.tensor_copy(out=logits[:], in_=logits_bf[:].rearrange("p b (t k) -> p (b t) k", k=3))
+        top = consts.tile([P, groups], F32, name="top")
+        nc.vector.tensor_reduce(out=top[:], in_=logits[:], axis=AXIS.X, op=ALU.max)
+        nc.vector.tensor_tensor(
+            out=logits[:], in0=logits[:], in1=top[:].unsqueeze(2).to_broadcast([P, groups, 3]), op=ALU.subtract
+        )
+        expd = consts.tile([P, groups, 3], F32, name="expd")
+        nc.scalar.activation(out=expd[:], in_=logits[:], func=ACT.Exp)
+        total = consts.tile([P, groups], F32, name="total")
+        nc.vector.tensor_reduce(out=total[:], in_=expd[:], axis=AXIS.X, op=ALU.add)
+        inverse = consts.tile([P, groups], F32, name="inverse")
+        nc.vector.reciprocal(out=inverse[:], in_=total[:])
+        gate = consts.tile([P, groups, 3], F32, name="gate")
+        nc.vector.tensor_tensor(
+            out=gate[:], in0=expd[:], in1=inverse[:].unsqueeze(2).to_broadcast([P, groups, 3]), op=ALU.mult
+        )
+        by_image = gate[:].rearrange("p (b t) k -> p b t k", t=PACK)
+        shift = consts.tile([P, groups], F32, name="shift")
+        shift_w = consts.tile([P, groups], F32, name="shift_w")
+        nc.vector.tensor_tensor(
+            out=shift[:].rearrange("p (b t) -> p b t", t=PACK), in0=by_image[:, :, :, 0],
+            in1=bias_h[:].unsqueeze(1).to_broadcast([P, IMAGES, PACK]), op=ALU.mult,
+        )
+        nc.vector.tensor_tensor(
+            out=shift_w[:].rearrange("p (b t) -> p b t", t=PACK), in0=by_image[:, :, :, 1],
+            in1=bias_w[:].unsqueeze(1).to_broadcast([P, IMAGES, PACK]), op=ALU.mult,
+        )
+        nc.vector.tensor_tensor(out=shift[:], in0=shift[:], in1=shift_w[:], op=ALU.add)
+
+        weights = {}
+        turned_tokens = {}
+        token_codes = {}
+        fused = {}
+        fused_codes = {}
+        part_w = {}
+        part_hc = {}
+        for branch in BRANCHES:
+            weights[branch] = quantise(turn(raw_weights[branch], NEIGHBOURS, True), consts, "weight_" + branch)
+            turn_tokens(0, branch, True)
+            quantise_tokens(0, branch)
+        for branch in BRANCHES:
+            turn_tokens(1, branch, True)
+
+        for n in range(TILES):
+            part_w[n] = blend_pool.tile([P, PACK, TILE_PIXELS], F32, tag="part_w", name="part_w")
+            part_hc[n] = blend_pool.tile([P, PACK, TILE_PIXELS], F32, tag="part_hc", name="part_hc")
+            fused[n] = blend_pool.tile([P, TILE_PIXELS * PACK], BF16, tag="fused", name="fused", align_bytes=64)
+            for t in range(PACK):
+                project(n, t)
+                if t == 0 and n > 0:
+                    fused_codes[n - 1] = quantise(fused[n - 1], blend_pool, "f")
+                if t < len(BRANCHES):
+                    quantise_tokens(n + 1, BRANCHES[t])
+            add_parts(nc.gpsimd, n, 0, GPSIMD_PIXELS)
+            if n == 0:
+                turned_wp = turn(raw_weights["p"], NEIGHBOURS, True)
+            for branch in BRANCHES:
+                turn_tokens(n + 2, branch, n == 0)
+            if n > 0:
+                output(n - 1)
+            add_parts(nc.vector, n, GPSIMD_PIXELS, TILE_PIXELS)
+            if n == 0:
+                weights["p"] = quantise(turned_wp, consts, "weight_p")
+        fused_codes[TILES - 1] = quantise(fused[TILES - 1], blend_pool, "f")
+        output(TILES - 1)

@@ -23,8 +23,9 @@ TILE_PIXELS = TILE_SLOTS * P
 TILES = IMAGES * SLOTS // TILE_SLOTS
 BRANCHES = ("h", "w", "c")
 RAW_BUFS = 4
-STORE_SLOTS = 1
-GPSIMD_PIXELS = 224
+GPSIMD_PIXELS = 512
+LAST_GPSIMD_PIXELS = 256
+GPSIMD_RUN = 128
 
 FLOPS = 4 * 2 * IMAGES * RES * RES * C * C
 
@@ -39,7 +40,7 @@ def tile_dynamixerblock_pb_kernel(
     with ctx:
         consts = ctx.enter_context(tc.tile_pool(name="consts", bufs=1))
         raw_pool = ctx.enter_context(tc.tile_pool(name="raw", bufs=RAW_BUFS))
-        grouped_pool = ctx.enter_context(tc.tile_pool(name="grouped", bufs=4))
+        grouped_pool = ctx.enter_context(tc.tile_pool(name="grouped", bufs=6))
         token_pool = ctx.enter_context(tc.tile_pool(name="tokens", bufs=2))
         blend_pool = ctx.enter_context(tc.tile_pool(name="blend", bufs=2))
         out_pool = ctx.enter_context(tc.tile_pool(name="results", bufs=6))
@@ -141,29 +142,26 @@ def tile_dynamixerblock_pb_kernel(
                 op=ALU.add,
             )
 
-        def output(n):
+        def output(n, s):
             image, half = divmod(n, SLOTS // TILE_SLOTS)
             codes, scales = fused_codes[n]
-            for first in range(0, TILE_SLOTS, STORE_SLOTS):
-                result = out_pool.tile([P, STORE_SLOTS, C], F32, tag="result", name="result")
-                for s in range(STORE_SLOTS):
-                    pixels = slice((first + s) * P, (first + s + 1) * P)
-                    acc = psum.tile([P, C], F32, tag="bank", name="acc_out")
-                    nc.tensor.matmul_mx(
-                        out=acc[:],
-                        lhsT=codes[:, pixels].bitcast(FP8X4),
-                        lhsT_scale=scales[:, pixels],
-                        rhs=weights["p"][0][:].bitcast(FP8X4),
-                        rhs_scale=weights["p"][1][:],
-                        start=True,
-                        stop=True,
-                    )
-                    nc.vector.tensor_tensor(out=result[:, s, :], in0=acc[:], in1=bp_all[:], op=ALU.add)
-                slot = half * TILE_SLOTS + first
-                nc.sync.dma_start(
-                    out=out[image].rearrange("i (q s) e -> (i q) s e", s=SLOTS)[:, slot : slot + STORE_SLOTS, :],
-                    in_=result[:],
-                )
+            pixels = slice(s * P, (s + 1) * P)
+            acc = psum.tile([P, C], F32, tag="bank", name="acc_out")
+            nc.tensor.matmul_mx(
+                out=acc[:],
+                lhsT=codes[:, pixels].bitcast(FP8X4),
+                lhsT_scale=scales[:, pixels],
+                rhs=weights["p"][0][:].bitcast(FP8X4),
+                rhs_scale=weights["p"][1][:],
+                start=True,
+                stop=True,
+            )
+            result = out_pool.tile([P, C], F32, tag="result", name="result")
+            nc.vector.tensor_tensor(out=result[:], in0=acc[:], in1=bp_all[:], op=ALU.add)
+            nc.sync.dma_start(
+                out=out[image].rearrange("i (q s) e -> (i q) s e", s=SLOTS)[:, half * TILE_SLOTS + s, :],
+                in_=result[:],
+            )
 
         ident = consts.tile([P, P], F32, name="ident")
         make_identity(nc, ident[:])
@@ -237,25 +235,29 @@ def tile_dynamixerblock_pb_kernel(
         for branch in BRANCHES:
             turn_tokens(1, branch, True)
 
-        for n in range(TILES):
-            part_w[n] = blend_pool.tile([P, PACK, TILE_PIXELS], F32, tag="part_w", name="part_w")
-            part_hc[n] = blend_pool.tile([P, PACK, TILE_PIXELS], F32, tag="part_hc", name="part_hc")
-            fused[n] = blend_pool.tile([P, TILE_PIXELS * PACK], BF16, tag="fused", name="fused", align_bytes=64)
+        for n in range(TILES + 2):
+            if 0 < n <= TILES:
+                gpsimd_pixels = GPSIMD_PIXELS if n < TILES else LAST_GPSIMD_PIXELS
+                fused[n - 1] = blend_pool.tile(
+                    [P, TILE_PIXELS * PACK], BF16, tag="fused", name="fused", align_bytes=64, bufs=1
+                )
+                for first in range(0, gpsimd_pixels, GPSIMD_RUN):
+                    add_parts(nc.gpsimd, n - 1, first, first + GPSIMD_RUN)
+            if n < TILES:
+                part_w[n] = blend_pool.tile([P, PACK, TILE_PIXELS], F32, tag="part_w", name="part_w")
+                part_hc[n] = blend_pool.tile([P, PACK, TILE_PIXELS], F32, tag="part_hc", name="part_hc")
             for t in range(PACK):
-                project(n, t)
-                if t == 0 and n > 0:
-                    fused_codes[n - 1] = quantise(fused[n - 1], blend_pool, "f")
-                if t < len(BRANCHES):
-                    quantise_tokens(n + 1, BRANCHES[t])
-            add_parts(nc.gpsimd, n, 0, GPSIMD_PIXELS)
-            if n == 0:
-                turned_wp = turn(raw_weights["p"], NEIGHBOURS, True)
+                if n < TILES:
+                    project(n, t)
+                if n >= 2:
+                    output(n - 2, t)
+            for branch in BRANCHES:
+                quantise_tokens(n + 1, branch)
             for branch in BRANCHES:
                 turn_tokens(n + 2, branch, n == 0)
-            if n > 0:
-                output(n - 1)
-            add_parts(nc.vector, n, GPSIMD_PIXELS, TILE_PIXELS)
             if n == 0:
-                weights["p"] = quantise(turned_wp, consts, "weight_p")
-        fused_codes[TILES - 1] = quantise(fused[TILES - 1], blend_pool, "f")
-        output(TILES - 1)
+                weights["p"] = quantise(turn(raw_weights["p"], NEIGHBOURS, True), consts, "weight_p")
+            if 0 < n <= TILES:
+                if gpsimd_pixels < TILE_PIXELS:
+                    add_parts(nc.vector, n - 1, gpsimd_pixels, TILE_PIXELS)
+                fused_codes[n - 1] = quantise(fused[n - 1], blend_pool, "f")

@@ -23,9 +23,9 @@ TILE_PIXELS = TILE_SLOTS * P
 TILES = IMAGES * SLOTS // TILE_SLOTS
 BRANCHES = ("h", "w", "c")
 RAW_BUFS = 4
-GPSIMD_PIXELS = 512
-LAST_GPSIMD_PIXELS = 256
-GPSIMD_RUN = 128
+GPSIMD_PIXELS = 320
+LAST_GPSIMD_PIXELS = 192
+GPSIMD_RUN = 64
 
 FLOPS = 4 * 2 * IMAGES * RES * RES * C * C
 
@@ -253,11 +253,11 @@ def tile_dynamixerblock_pb_kernel(
                     output(n - 2, t)
             for branch in BRANCHES:
                 quantise_tokens(n + 1, branch)
+                if branch == "h" and 0 < n <= TILES:
+                    add_parts(nc.vector, n - 1, gpsimd_pixels, TILE_PIXELS)
             for branch in BRANCHES:
                 turn_tokens(n + 2, branch, n == 0)
             if n == 0:
                 weights["p"] = quantise(turn(raw_weights["p"], NEIGHBOURS, True), consts, "weight_p")
             if 0 < n <= TILES:
-                if gpsimd_pixels < TILE_PIXELS:
-                    add_parts(nc.vector, n - 1, gpsimd_pixels, TILE_PIXELS)
                 fused_codes[n - 1] = quantise(fused[n - 1], blend_pool, "f")

@@ -23,9 +23,9 @@ TILE_PIXELS = TILE_SLOTS * P
 TILES = IMAGES * SLOTS // TILE_SLOTS
 BRANCHES = ("h", "w", "c")
 RAW_BUFS = 4
-GPSIMD_PIXELS = 320
-LAST_GPSIMD_PIXELS = 192
-GPSIMD_RUN = 64
+HALF_PIXELS = TILE_PIXELS // 2
+LAST_GPSIMD_PIXELS = 64
+GPSIMD_PIXELS = 160
 
 FLOPS = 4 * 2 * IMAGES * RES * RES * C * C
 
@@ -40,7 +40,7 @@ def tile_dynamixerblock_pb_kernel(
     with ctx:
         consts = ctx.enter_context(tc.tile_pool(name="consts", bufs=1))
         raw_pool = ctx.enter_context(tc.tile_pool(name="raw", bufs=RAW_BUFS))
-        grouped_pool = ctx.enter_context(tc.tile_pool(name="grouped", bufs=6))
+        grouped_pool = ctx.enter_context(tc.tile_pool(name="grouped", bufs=8))
         token_pool = ctx.enter_context(tc.tile_pool(name="tokens", bufs=2))
         blend_pool = ctx.enter_context(tc.tile_pool(name="blend", bufs=2))
         out_pool = ctx.enter_context(tc.tile_pool(name="results", bufs=6))
@@ -71,81 +71,93 @@ def tile_dynamixerblock_pb_kernel(
             nc.sync.dma_start(out=raw[:].rearrange("p (s k) -> p s k", s=PACK), in_=rows)
             return raw
 
-        def turn(raw, word_order, vector_helps):
-            words = raw[:].bitcast(F32).rearrange(word_order, s=4, u=2)
-            grouped = grouped_pool.tile([P, 4 * P * PACK], BF16, tag="grouped", name="grouped", align_bytes=64)
+        def turn_bank(raw, grouped, half, engine_copy):
+            words = raw[:].bitcast(F32).rearrange(NEIGHBOURS, s=4, u=2)
             pairs = grouped[:].bitcast(F32).rearrange("p (c u) -> p c u", u=2)
-            for half in range(2):
-                bank = psum.tile([P, 2, 2 * P], F32, tag="bank", name="turned")
-                for s in range(2):
-                    for u in range(2):
-                        nc.tensor.transpose(bank[:, u, s * P : (s + 1) * P], words[:, 2 * half + s, u, :], ident[:])
-                target = pairs[:, half * 2 * P : (half + 1) * 2 * P, :]
-                source = bank[:].rearrange("p u c -> p c u")
-                if vector_helps and half == 1:
-                    nc.vector.tensor_copy(out=target, in_=source)
-                else:
-                    nc.scalar.copy(out=target, in_=source)
+            bank = psum.tile([P, 2, 2 * P], F32, tag="bank", name="turned")
+            for s in range(2):
+                for u in range(2):
+                    nc.tensor.transpose(bank[:, u, s * P : (s + 1) * P], words[:, 2 * half + s, u, :], ident[:])
+            engine_copy(
+                out=pairs[:, half * 2 * P : (half + 1) * 2 * P, :],
+                in_=bank[:].rearrange("p u c -> p c u"),
+            )
+
+        def new_grouped():
+            return grouped_pool.tile([P, 4 * P * PACK], BF16, tag="grouped", name="grouped", align_bytes=64)
+
+        def turn(raw):
+            grouped = new_grouped()
+            turn_bank(raw, grouped, 0, nc.scalar.copy)
+            turn_bank(raw, grouped, 1, nc.vector.tensor_copy)
             return grouped
 
-        def quantise(grouped, pool, name):
-            codes = pool.tile([P, 4 * P], U32, tag="codes_" + name, name="codes_" + name, align_bytes=64)
-            scales = pool.tile([P, 4 * P], U8, tag="scales_" + name, name="scales_" + name, align_bytes=64)
+        def quantise(grouped, pool, name, columns=4 * P):
+            codes = pool.tile([P, columns], U32, tag="codes_" + name, name="codes_" + name, align_bytes=64)
+            scales = pool.tile([P, columns], U8, tag="scales_" + name, name="scales_" + name, align_bytes=64)
             nc.vector.quantize_mx(out=codes[:].bitcast(FP8X4), scales=scales[:], in_=grouped[:])
             return codes, scales
 
-        def turn_tokens(n, branch, vector_helps):
+        def turn_tokens_bank(n, bank, engine_copy):
             if n < TILES:
-                turned_tokens[(n, branch)] = turn(raw_tokens[(n, branch)], NEIGHBOURS, vector_helps)
-                if n + RAW_BUFS < TILES:
+                branch = BRANCHES[bank // 2]
+                if bank % 2 == 0:
+                    turned_tokens[(n, branch)] = new_grouped()
+                turn_bank(raw_tokens[(n, branch)], turned_tokens[(n, branch)], bank % 2, engine_copy)
+                if bank % 2 == 1 and n + RAW_BUFS < TILES:
                     raw_tokens[(n + RAW_BUFS, branch)] = load_tokens(n + RAW_BUFS, branch)
 
         def quantise_tokens(n, branch):
             if n < TILES:
                 token_codes[(n, branch)] = quantise(turned_tokens[(n, branch)], token_pool, branch)
 
-        def project(n, t):
+        def project(n, t, branch):
             column = (n * TILE_SLOTS // SLOTS) * PACK + t
             channels = slice(t * P, (t + 1) * P)
-            acc = {}
-            for branch in BRANCHES:
-                codes, scales = token_codes[(n, branch)]
-                acc[branch] = psum.tile([P, TILE_PIXELS], F32, tag="bank", name="acc_" + branch)
-                nc.tensor.matmul_mx(
-                    out=acc[branch][:],
-                    lhsT=weights[branch][0][:, channels].bitcast(FP8X4),
-                    lhsT_scale=weights[branch][1][:, channels],
-                    rhs=codes[:].bitcast(FP8X4),
-                    rhs_scale=scales[:],
-                    start=True,
-                    stop=True,
+            codes, scales = token_codes[(n, branch)]
+            acc = psum.tile([P, TILE_PIXELS], F32, tag="bank", name="acc_" + branch)
+            nc.tensor.matmul_mx(
+                out=acc[:],
+                lhsT=weights[branch][0][:, channels].bitcast(FP8X4),
+                lhsT_scale=weights[branch][1][:, channels],
+                rhs=codes[:].bitcast(FP8X4),
+                rhs_scale=scales[:],
+                start=True,
+                stop=True,
+            )
+            if branch == "h":
+                nc.scalar.activation(
+                    out=part_h[n][:, t, :], in_=acc[:], func=ACT.Identity,
+                    scale=gate[:, column, 0:1], bias=shift[:, column : column + 1],
                 )
-            part_h = blend_pool.tile([P, TILE_PIXELS], F32, tag="part_h", name="part_h", bufs=3)
-            nc.scalar.activation(
-                out=part_h[:], in_=acc["h"][:], func=ACT.Identity,
-                scale=gate[:, column, 0:1], bias=shift[:, column : column + 1],
-            )
-            nc.scalar.activation(
-                out=part_w[n][:, t, :], in_=acc["w"][:], func=ACT.Copy, scale=gate[:, column, 1:2]
-            )
-            nc.vector.scalar_tensor_tensor(
-                out=part_hc[n][:, t, :], in0=acc["c"][:], scalar=gate[:, column, 2:3], in1=part_h[:],
-                op0=ALU.mult, op1=ALU.add,
-            )
+            elif branch == "w":
+                nc.scalar.activation(out=part_w[n][:, t, :], in_=acc[:], func=ACT.Copy, scale=gate[:, column, 1:2])
+            else:
+                nc.vector.scalar_tensor_tensor(
+                    out=part_hc[n][:, t, :], in0=acc[:], scalar=gate[:, column, 2:3], in1=part_h[n][:, t, :],
+                    op0=ALU.mult, op1=ALU.add,
+                )
 
-        def add_parts(engine, n, first, last):
+        def new_parts(n):
+            part_h[n] = blend_pool.tile([P, PACK, TILE_PIXELS], F32, tag="part_h", name="part_h")
+            part_w[n] = blend_pool.tile([P, PACK, TILE_PIXELS], F32, tag="part_w", name="part_w")
+            part_hc[n] = blend_pool.tile([P, PACK, TILE_PIXELS], F32, tag="part_hc", name="part_hc")
+
+        def add_parts(engine, n, half, first, last):
             runs = slice(first // 4, last // 4)
+            begin = half * HALF_PIXELS // 4
+            source = slice(begin + first // 4, begin + last // 4)
             engine.tensor_tensor(
-                out=fused[n][:].rearrange("p (c i t) -> p c t i", i=4, t=PACK)[:, runs, :, :],
-                in0=part_hc[n][:].rearrange("p t (c i) -> p c t i", i=4)[:, runs, :, :],
-                in1=part_w[n][:].rearrange("p t (c i) -> p c t i", i=4)[:, runs, :, :],
+                out=fused[(n, half)][:].rearrange("p (c i t) -> p c t i", i=4, t=PACK)[:, runs, :, :],
+                in0=part_hc[n][:].rearrange("p t (c i) -> p c t i", i=4)[:, source, :, :],
+                in1=part_w[n][:].rearrange("p t (c i) -> p c t i", i=4)[:, source, :, :],
                 op=ALU.add,
             )
 
         def output(n, s):
             image, half = divmod(n, SLOTS // TILE_SLOTS)
-            codes, scales = fused_codes[n]
-            pixels = slice(s * P, (s + 1) * P)
+            codes, scales = fused_codes[(n, s // 2)]
+            pixels = slice(s % 2 * P, (s % 2 + 1) * P)
             acc = psum.tile([P, C], F32, tag="bank", name="acc_out")
             nc.tensor.matmul_mx(
                 out=acc[:],
@@ -192,72 +204,109 @@ def tile_dynamixerblock_pb_kernel(
 
         groups = IMAGES * PACK
         logits = consts.tile([P, groups, 3], F32, name="logits")
-        nc.vector.tensor_copy(out=logits[:], in_=logits_bf[:].rearrange("p b (t k) -> p (b t) k", k=3))
         top = consts.tile([P, groups], F32, name="top")
+        expd = consts.tile([P, groups, 3], F32, name="expd")
+        total = consts.tile([P, groups], F32, name="total")
+        inverse = consts.tile([P, groups], F32, name="inverse")
+        gate = consts.tile([P, groups, 3], F32, name="gate")
+        by_image = gate[:].rearrange("p (b t) k -> p b t k", t=PACK)
+        shift = consts.tile([P, groups], F32, name="shift")
+        shift_w = consts.tile([P, groups], F32, name="shift_w")
+        nc.vector.tensor_copy(out=logits[:], in_=logits_bf[:].rearrange("p b (t k) -> p (b t) k", k=3))
         nc.vector.tensor_reduce(out=top[:], in_=logits[:], axis=AXIS.X, op=ALU.max)
         nc.vector.tensor_tensor(
             out=logits[:], in0=logits[:], in1=top[:].unsqueeze(2).to_broadcast([P, groups, 3]), op=ALU.subtract
         )
-        expd = consts.tile([P, groups, 3], F32, name="expd")
         nc.scalar.activation(out=expd[:], in_=logits[:], func=ACT.Exp)
-        total = consts.tile([P, groups], F32, name="total")
-        nc.vector.tensor_reduce(out=total[:], in_=expd[:], axis=AXIS.X, op=ALU.add)
-        inverse = consts.tile([P, groups], F32, name="inverse")
-        nc.vector.reciprocal(out=inverse[:], in_=total[:])
-        gate = consts.tile([P, groups, 3], F32, name="gate")
-        nc.vector.tensor_tensor(
-            out=gate[:], in0=expd[:], in1=inverse[:].unsqueeze(2).to_broadcast([P, groups, 3]), op=ALU.mult
-        )
-        by_image = gate[:].rearrange("p (b t) k -> p b t k", t=PACK)
-        shift = consts.tile([P, groups], F32, name="shift")
-        shift_w = consts.tile([P, groups], F32, name="shift_w")
-        nc.vector.tensor_tensor(
-            out=shift[:].rearrange("p (b t) -> p b t", t=PACK), in0=by_image[:, :, :, 0],
-            in1=bias_h[:].unsqueeze(1).to_broadcast([P, IMAGES, PACK]), op=ALU.mult,
-        )
-        nc.vector.tensor_tensor(
-            out=shift_w[:].rearrange("p (b t) -> p b t", t=PACK), in0=by_image[:, :, :, 1],
-            in1=bias_w[:].unsqueeze(1).to_broadcast([P, IMAGES, PACK]), op=ALU.mult,
-        )
-        nc.vector.tensor_tensor(out=shift[:], in0=shift[:], in1=shift_w[:], op=ALU.add)
+
+        def softmax_step(step):
+            if step == 0:
+                nc.vector.tensor_reduce(out=total[:], in_=expd[:], axis=AXIS.X, op=ALU.add)
+            elif step == 1:
+                nc.vector.reciprocal(out=inverse[:], in_=total[:])
+            elif step == 2:
+                nc.vector.tensor_tensor(
+                    out=gate[:], in0=expd[:], in1=inverse[:].unsqueeze(2).to_broadcast([P, groups, 3]), op=ALU.mult
+                )
+            elif step == 3:
+                nc.vector.tensor_tensor(
+                    out=shift[:].rearrange("p (b t) -> p b t", t=PACK), in0=by_image[:, :, :, 0],
+                    in1=bias_h[:].unsqueeze(1).to_broadcast([P, IMAGES, PACK]), op=ALU.mult,
+                )
+                nc.vector.tensor_tensor(
+                    out=shift_w[:].rearrange("p (b t) -> p b t", t=PACK), in0=by_image[:, :, :, 1],
+                    in1=bias_w[:].unsqueeze(1).to_broadcast([P, IMAGES, PACK]), op=ALU.mult,
+                )
+            elif step == 4:
+                nc.vector.tensor_tensor(out=shift[:], in0=shift[:], in1=shift_w[:], op=ALU.add)
 
         weights = {}
         turned_tokens = {}
         token_codes = {}
         fused = {}
         fused_codes = {}
+        part_h = {}
         part_w = {}
         part_hc = {}
-        for branch in BRANCHES:
-            weights[branch] = quantise(turn(raw_weights[branch], NEIGHBOURS, True), consts, "weight_" + branch)
-            turn_tokens(0, branch, True)
+        new_parts(0)
+        turned_weights = {}
+        def ready_branch(branch):
+            turned_weights[branch] = turn(raw_weights[branch])
+            if branch == "h":
+                softmax_step(3)
+            weights[branch] = quantise(turned_weights[branch], consts, "weight_" + branch)
+            if branch == "h":
+                softmax_step(4)
+            turned_tokens[(0, branch)] = turn(raw_tokens[(0, branch)])
+            raw_tokens[(RAW_BUFS, branch)] = load_tokens(RAW_BUFS, branch)
             quantise_tokens(0, branch)
-        for branch in BRANCHES:
-            turn_tokens(1, branch, True)
 
-        for n in range(TILES + 2):
-            if 0 < n <= TILES:
-                gpsimd_pixels = GPSIMD_PIXELS if n < TILES else LAST_GPSIMD_PIXELS
-                fused[n - 1] = blend_pool.tile(
-                    [P, TILE_PIXELS * PACK], BF16, tag="fused", name="fused", align_bytes=64, bufs=1
+        for step in range(3):
+            softmax_step(step)
+        ready_branch("h")
+        ready_branch("w")
+        for t in range(PACK):
+            project(0, t, "h")
+        ready_branch("c")
+        for t in range(PACK):
+            project(0, t, "w")
+        for bank in range(3):
+            turn_tokens_bank(1, bank, nc.scalar.copy)
+        for t in range(PACK):
+            project(0, t, "c")
+
+        for step in range(2 * TILES + 4):
+            n, half = divmod(step, 2)
+            blend = 0 < n <= TILES
+            gpsimd_pixels = GPSIMD_PIXELS if n < TILES else LAST_GPSIMD_PIXELS
+            if blend:
+                fused[(n - 1, half)] = blend_pool.tile(
+                    [P, HALF_PIXELS * PACK], BF16, tag="fused", name="fused", align_bytes=64, bufs=1
                 )
-                for first in range(0, gpsimd_pixels, GPSIMD_RUN):
-                    add_parts(nc.gpsimd, n - 1, first, first + GPSIMD_RUN)
-            if n < TILES:
-                part_w[n] = blend_pool.tile([P, PACK, TILE_PIXELS], F32, tag="part_w", name="part_w")
-                part_hc[n] = blend_pool.tile([P, PACK, TILE_PIXELS], F32, tag="part_hc", name="part_hc")
-            for t in range(PACK):
-                if n < TILES:
-                    project(n, t)
-                if n >= 2:
-                    output(n - 2, t)
-            for branch in BRANCHES:
-                quantise_tokens(n + 1, branch)
-                if branch == "h" and 0 < n <= TILES:
-                    add_parts(nc.vector, n - 1, gpsimd_pixels, TILE_PIXELS)
-            for branch in BRANCHES:
-                turn_tokens(n + 2, branch, n == 0)
-            if n == 0:
-                weights["p"] = quantise(turn(raw_weights["p"], NEIGHBOURS, True), consts, "weight_p")
-            if 0 < n <= TILES:
-                fused_codes[n - 1] = quantise(fused[n - 1], blend_pool, "f")
+                add_parts(nc.gpsimd, n - 1, half, 0, gpsimd_pixels)
+            if 0 < n < TILES and half == 0:
+                new_parts(n)
+            done = step - 4
+            if done >= 0:
+                for t in range(2):
+                    output(done // 2, done % 2 * 2 + t)
+            if 0 < n < TILES:
+                for branch in ("h", "c", "w"):
+                    for t in range(2):
+                        project(n, 2 * half + t, branch)
+            ahead, ahead_half = divmod(step + 3, 2)
+            for bank in range(3):
+                turn_tokens_bank(
+                    ahead, ahead_half * 3 + bank, nc.vector.tensor_copy if n == 0 and bank == 1 else nc.scalar.copy
+                )
+            if step == 0:
+                turned_wp = turn(raw_weights["p"])
+            quantise_tokens(n + 1, "h" if half == 0 else "w")
+            if blend:
+                add_parts(nc.vector, n - 1, half, gpsimd_pixels, HALF_PIXELS)
+            if half == 1:
+                quantise_tokens(n + 1, "c")
+            if step == 0:
+                weights["p"] = quantise(turned_wp, consts, "weight_p")
+            if blend:
+                fused_codes[(n - 1, half)] = quantise(fused[(n - 1, half)], blend_pool, "f", HALF_PIXELS)

@@ -71,13 +71,16 @@ def tile_dynamixerblock_pb_kernel(
             nc.sync.dma_start(out=raw[:].rearrange("p (s k) -> p s k", s=PACK), in_=rows)
             return raw
 
-        def turn_bank(raw, grouped, half, engine_copy):
+        def turn_bank(raw, half):
             words = raw[:].bitcast(F32).rearrange(NEIGHBOURS, s=4, u=2)
-            pairs = grouped[:].bitcast(F32).rearrange("p (c u) -> p c u", u=2)
             bank = psum.tile([P, 2, 2 * P], F32, tag="bank", name="turned")
             for s in range(2):
                 for u in range(2):
                     nc.tensor.transpose(bank[:, u, s * P : (s + 1) * P], words[:, 2 * half + s, u, :], ident[:])
+            return bank
+
+        def empty_bank(bank, grouped, half, engine_copy):
+            pairs = grouped[:].bitcast(F32).rearrange("p (c u) -> p c u", u=2)
             engine_copy(
                 out=pairs[:, half * 2 * P : (half + 1) * 2 * P, :],
                 in_=bank[:].rearrange("p u c -> p c u"),
@@ -88,8 +91,8 @@ def tile_dynamixerblock_pb_kernel(
 
         def turn(raw):
             grouped = new_grouped()
-            turn_bank(raw, grouped, 0, nc.scalar.copy)
-            turn_bank(raw, grouped, 1, nc.vector.tensor_copy)
+            for half, engine_copy in ((0, nc.scalar.copy), (1, nc.vector.tensor_copy)):
+                empty_bank(turn_bank(raw, half), grouped, half, engine_copy)
             return grouped
 
         def quantise(grouped, pool, name, columns=4 * P):
@@ -103,7 +106,8 @@ def tile_dynamixerblock_pb_kernel(
                 branch = BRANCHES[bank // 2]
                 if bank % 2 == 0:
                     turned_tokens[(n, branch)] = new_grouped()
-                turn_bank(raw_tokens[(n, branch)], turned_tokens[(n, branch)], bank % 2, engine_copy)
+                turned = turn_bank(raw_tokens[(n, branch)], bank % 2)
+                empty_bank(turned, turned_tokens[(n, branch)], bank % 2, engine_copy)
                 if bank % 2 == 1 and n + RAW_BUFS < TILES:
                     raw_tokens[(n + RAW_BUFS, branch)] = load_tokens(n + RAW_BUFS, branch)
 
@@ -112,7 +116,6 @@ def tile_dynamixerblock_pb_kernel(
                 token_codes[(n, branch)] = quantise(turned_tokens[(n, branch)], token_pool, branch)
 
         def project(n, t, branch):
-            column = (n * TILE_SLOTS // SLOTS) * PACK + t
             channels = slice(t * P, (t + 1) * P)
             codes, scales = token_codes[(n, branch)]
             acc = psum.tile([P, TILE_PIXELS], F32, tag="bank", name="acc_" + branch)
@@ -125,6 +128,10 @@ def tile_dynamixerblock_pb_kernel(
                 start=True,
                 stop=True,
             )
+            return acc
+
+        def weigh(acc, n, t, branch):
+            column = (n * TILE_SLOTS // SLOTS) * PACK + t
             if branch == "h":
                 nc.scalar.activation(
                     out=part_h[n][:, t, :], in_=acc[:], func=ACT.Identity,
@@ -265,15 +272,12 @@ def tile_dynamixerblock_pb_kernel(
             softmax_step(step)
         ready_branch("h")
         ready_branch("w")
-        for t in range(PACK):
-            project(0, t, "h")
         ready_branch("c")
-        for t in range(PACK):
-            project(0, t, "w")
+        for branch in BRANCHES:
+            for t in range(PACK):
+                weigh(project(0, t, branch), 0, t, branch)
         for bank in range(3):
-            turn_tokens_bank(1, bank, nc.scalar.copy)
-        for t in range(PACK):
-            project(0, t, "c")
+            turn_tokens_bank(1, bank, nc.vector.tensor_copy if bank == 1 else nc.scalar.copy)
 
         for step in range(2 * TILES + 4):
             n, half = divmod(step, 2)
@@ -293,7 +297,7 @@ def tile_dynamixerblock_pb_kernel(
             if 0 < n < TILES:
                 for branch in ("h", "c", "w"):
                     for t in range(2):
-                        project(n, 2 * half + t, branch)
+                        weigh(project(n, 2 * half + t, branch), n, 2 * half + t, branch)
             ahead, ahead_half = divmod(step + 3, 2)
             for bank in range(3):
                 turn_tokens_bank(

@@ -25,7 +25,7 @@ BRANCHES = ("h", "w", "c")
 RAW_BUFS = 4
 HALF_PIXELS = TILE_PIXELS // 2
 LAST_GPSIMD_PIXELS = 64
-GPSIMD_PIXELS = 160
+GPSIMD_PIXELS = 224
 
 FLOPS = 4 * 2 * IMAGES * RES * RES * C * C
 

@@ -22,10 +22,11 @@ TILE_SLOTS = 4
 TILE_PIXELS = TILE_SLOTS * P
 TILES = IMAGES * SLOTS // TILE_SLOTS
 BRANCHES = ("h", "w", "c")
+PROJECT_ORDER = ("h", "c", "w")
 RAW_BUFS = 4
 HALF_PIXELS = TILE_PIXELS // 2
 LAST_GPSIMD_PIXELS = 64
-GPSIMD_PIXELS = 224
+GPSIMD_PIXELS = 256
 
 FLOPS = 4 * 2 * IMAGES * RES * RES * C * C
 
@@ -40,7 +41,7 @@ def tile_dynamixerblock_pb_kernel(
     with ctx:
         consts = ctx.enter_context(tc.tile_pool(name="consts", bufs=1))
         raw_pool = ctx.enter_context(tc.tile_pool(name="raw", bufs=RAW_BUFS))
-        grouped_pool = ctx.enter_context(tc.tile_pool(name="grouped", bufs=8))
+        grouped_pool = ctx.enter_context(tc.tile_pool(name="grouped", bufs=10))
         token_pool = ctx.enter_context(tc.tile_pool(name="tokens", bufs=2))
         blend_pool = ctx.enter_context(tc.tile_pool(name="blend", bufs=2))
         out_pool = ctx.enter_context(tc.tile_pool(name="results", bufs=6))
@@ -91,8 +92,8 @@ def tile_dynamixerblock_pb_kernel(
 
         def turn(raw):
             grouped = new_grouped()
-            for half, engine_copy in ((0, nc.scalar.copy), (1, nc.vector.tensor_copy)):
-                empty_bank(turn_bank(raw, half), grouped, half, engine_copy)
+            for half in range(2):
+                empty_bank(turn_bank(raw, half), grouped, half, nc.scalar.copy)
             return grouped
 
         def quantise(grouped, pool, name, columns=4 * P):
@@ -270,47 +271,60 @@ def tile_dynamixerblock_pb_kernel(
 
         for step in range(3):
             softmax_step(step)
-        ready_branch("h")
-        ready_branch("w")
-        ready_branch("c")
-        for branch in BRANCHES:
+        for place, branch in enumerate(BRANCHES):
+            turned_weights[branch] = turn(raw_weights[branch])
+            if place > 0:
+                quantise_tokens(0, BRANCHES[place - 1])
+            else:
+                softmax_step(3)
+            turned_tokens[(0, branch)] = turn(raw_tokens[(0, branch)])
+            raw_tokens[(RAW_BUFS, branch)] = load_tokens(RAW_BUFS, branch)
+            weights[branch] = quantise(turned_weights[branch], consts, "weight_" + branch)
+            if place == 0:
+                softmax_step(4)
+        quantise_tokens(0, "c")
+        for branch in PROJECT_ORDER:
             for t in range(PACK):
                 weigh(project(0, t, branch), 0, t, branch)
+        for bank in range(6):
+            turn_tokens_bank(1, bank, nc.vector.tensor_copy if bank % 2 == 1 else nc.scalar.copy)
+            if bank in (3, 5):
+                quantise_tokens(1, BRANCHES[bank // 2 - 1])
+        turned_wp = turn(raw_weights["p"])
+        quantise_tokens(1, "c")
         for bank in range(3):
-            turn_tokens_bank(1, bank, nc.vector.tensor_copy if bank == 1 else nc.scalar.copy)
+            turn_tokens_bank(2, bank, nc.vector.tensor_copy if bank == 1 else nc.scalar.copy)
+        weights["p"] = quantise(turned_wp, consts, "weight_p")
 
-        for step in range(2 * TILES + 4):
+        for step in range(2, 2 * TILES + 4):
             n, half = divmod(step, 2)
-            blend = 0 < n <= TILES
+            blend = n <= TILES
             gpsimd_pixels = GPSIMD_PIXELS if n < TILES else LAST_GPSIMD_PIXELS
             if blend:
                 fused[(n - 1, half)] = blend_pool.tile(
                     [P, HALF_PIXELS * PACK], BF16, tag="fused", name="fused", align_bytes=64, bufs=1
                 )
                 add_parts(nc.gpsimd, n - 1, half, 0, gpsimd_pixels)
-            if 0 < n < TILES and half == 0:
+            if n < TILES and half == 0:
                 new_parts(n)
             done = step - 4
             if done >= 0:
                 for t in range(2):
                     output(done // 2, done % 2 * 2 + t)
-            if 0 < n < TILES:
-                for branch in ("h", "c", "w"):
+            if n < TILES:
+                for branch in PROJECT_ORDER:
                     for t in range(2):
                         weigh(project(n, 2 * half + t, branch), n, 2 * half + t, branch)
             ahead, ahead_half = divmod(step + 3, 2)
             for bank in range(3):
+                on_vector = half == 0 and bank == 0
                 turn_tokens_bank(
-                    ahead, ahead_half * 3 + bank, nc.vector.tensor_copy if n == 0 and bank == 1 else nc.scalar.copy
+                    ahead, ahead_half * 3 + bank, nc.vector.tensor_copy if on_vector else nc.scalar.copy
                 )
-            if step == 0:
-                turned_wp = turn(raw_weights["p"])
-            quantise_tokens(n + 1, "h" if half == 0 else "w")
-            if blend:
-                add_parts(nc.vector, n - 1, half, gpsimd_pixels, HALF_PIXELS)
             if half == 1:
-                quantise_tokens(n + 1, "c")
-            if step == 0:
-                weights["p"] = quantise(turned_wp, consts, "weight_p")
+                quantise_tokens(n + 1, "w")
+            if blend and gpsimd_pixels < HALF_PIXELS:
+                add_parts(nc.vector, n - 1, half, gpsimd_pixels, HALF_PIXELS)
+            quantise_tokens(n + 1, "h" if half == 0 else "c")
             if blend:
                 fused_codes[(n - 1, half)] = quantise(fused[(n - 1, half)], blend_pool, "f", HALF_PIXELS)

from contextlib import ExitStack

import concourse.mybir as mybir
from concourse.masks import make_identity

F32 = mybir.dt.float32
BF16 = mybir.dt.bfloat16
U32 = mybir.dt.uint32
U8 = mybir.dt.uint8
FP8X4 = mybir.dt.float8_e4m3fn_x4
ALU = mybir.AluOpType
ACT = mybir.ActivationFunctionType
AXIS = mybir.AxisListType

P = 128
PACK = 4
C = P * PACK
IMAGES = 4
RES = 32
SLOTS = RES * RES // P
TILE_SLOTS = 4
TILE_PIXELS = TILE_SLOTS * P
TILES = IMAGES * SLOTS // TILE_SLOTS
BRANCHES = ("h", "w", "c")
PROJECT_ORDER = ("h", "c", "w")
RAW_BUFS = 4
HALF_PIXELS = TILE_PIXELS // 2
LAST_GPSIMD_PIXELS = 64
GPSIMD_PIXELS = 256

FLOPS = 4 * 2 * IMAGES * RES * RES * C * C

NEIGHBOURS = "p (s q u) -> p s u q"


def tile_dynamixerblock_pb_kernel(
    tc, y_h, y_w, x, a_logits, Wo_h, bo_h, Wo_w, bo_w, Wmlpc, Wp, bp, out
):
    nc = tc.nc
    ctx = ExitStack()
    with ctx:
        consts = ctx.enter_context(tc.tile_pool(name="consts", bufs=1))
        raw_pool = ctx.enter_context(tc.tile_pool(name="raw", bufs=RAW_BUFS))
        grouped_pool = ctx.enter_context(tc.tile_pool(name="grouped", bufs=10))
        token_pool = ctx.enter_context(tc.tile_pool(name="tokens", bufs=2))
        blend_pool = ctx.enter_context(tc.tile_pool(name="blend", bufs=2))
        out_pool = ctx.enter_context(tc.tile_pool(name="results", bufs=6))
        psum = ctx.enter_context(tc.psum_pool(name="psum", bufs=8))
        ctx.enter_context(tc.manual_schedule())

        def load_tokens(n, branch):
            image, half = divmod(n, SLOTS // TILE_SLOTS)
            first = half * TILE_SLOTS
            raw = raw_pool.tile([P, TILE_SLOTS * C], BF16, tag="raw_" + branch, name="raw_" + branch)
            if branch == "h":
                for q in range(RES // SLOTS):
                    columns = y_h[image * RES + q * SLOTS + first : image * RES + q * SLOTS + first + TILE_SLOTS]
                    nc.sync.dma_start(
                        out=raw[q : P : RES // SLOTS, :].rearrange("i (s k) -> i s k", s=TILE_SLOTS),
                        in_=columns.rearrange("s i k -> i s k"),
                    )
            else:
                rows = y_w[image * RES : (image + 1) * RES] if branch == "w" else x[image]
                nc.sync.dma_start(
                    out=raw[:].rearrange("p (s k) -> p s k", s=TILE_SLOTS),
                    in_=rows.rearrange("i (q s) k -> (i q) s k", s=SLOTS)[:, first : first + TILE_SLOTS, :],
                )
            return raw

        def load_weight(rows, name):
            raw = raw_pool.tile([P, PACK * C], BF16, tag="raw_weight", name="raw_" + name)
            nc.sync.dma_start(out=raw[:].rearrange("p (s k) -> p s k", s=PACK), in_=rows)
            return raw

        def turn_bank(raw, half):
            words = raw[:].bitcast(F32).rearrange(NEIGHBOURS, s=4, u=2)
            bank = psum.tile([P, 2, 2 * P], F32, tag="bank", name="turned")
            for s in range(2):
                for u in range(2):
                    nc.tensor.transpose(bank[:, u, s * P : (s + 1) * P], words[:, 2 * half + s, u, :], ident[:])
            return bank

        def empty_bank(bank, grouped, half, engine_copy):
            pairs = grouped[:].bitcast(F32).rearrange("p (c u) -> p c u", u=2)
            engine_copy(
                out=pairs[:, half * 2 * P : (half + 1) * 2 * P, :],
                in_=bank[:].rearrange("p u c -> p c u"),
            )

        def new_grouped():
            return grouped_pool.tile([P, 4 * P * PACK], BF16, tag="grouped", name="grouped", align_bytes=64)

        def turn(raw):
            grouped = new_grouped()
            for half in range(2):
                empty_bank(turn_bank(raw, half), grouped, half, nc.scalar.copy)
            return grouped

        def quantise(grouped, pool, name, columns=4 * P):
            codes = pool.tile([P, columns], U32, tag="codes_" + name, name="codes_" + name, align_bytes=64)
            scales = pool.tile([P, columns], U8, tag="scales_" + name, name="scales_" + name, align_bytes=64)
            nc.vector.quantize_mx(out=codes[:].bitcast(FP8X4), scales=scales[:], in_=grouped[:])
            return codes, scales

        def turn_tokens_bank(n, bank, engine_copy):
            if n < TILES:
                branch = BRANCHES[bank // 2]
                if bank % 2 == 0:
                    turned_tokens[(n, branch)] = new_grouped()
                turned = turn_bank(raw_tokens[(n, branch)], bank % 2)
                empty_bank(turned, turned_tokens[(n, branch)], bank % 2, engine_copy)
                if bank % 2 == 1 and n + RAW_BUFS < TILES:
                    raw_tokens[(n + RAW_BUFS, branch)] = load_tokens(n + RAW_BUFS, branch)

        def quantise_tokens(n, branch):
            if n < TILES:
                token_codes[(n, branch)] = quantise(turned_tokens[(n, branch)], token_pool, branch)

        def project(n, t, branch):
            channels = slice(t * P, (t + 1) * P)
            codes, scales = token_codes[(n, branch)]
            acc = psum.tile([P, TILE_PIXELS], F32, tag="bank", name="acc_" + branch)
            nc.tensor.matmul_mx(
                out=acc[:],
                lhsT=weights[branch][0][:, channels].bitcast(FP8X4),
                lhsT_scale=weights[branch][1][:, channels],
                rhs=codes[:].bitcast(FP8X4),
                rhs_scale=scales[:],
                start=True,
                stop=True,
            )
            return acc

        def weigh(acc, n, t, branch):
            column = (n * TILE_SLOTS // SLOTS) * PACK + t
            if branch == "h":
                nc.scalar.activation(
                    out=part_h[n][:, t, :], in_=acc[:], func=ACT.Identity,
                    scale=gate[:, column, 0:1], bias=shift[:, column : column + 1],
                )
            elif branch == "w":
                nc.scalar.activation(out=part_w[n][:, t, :], in_=acc[:], func=ACT.Copy, scale=gate[:, column, 1:2])
            else:
                nc.vector.scalar_tensor_tensor(
                    out=part_hc[n][:, t, :], in0=acc[:], scalar=gate[:, column, 2:3], in1=part_h[n][:, t, :],
                    op0=ALU.mult, op1=ALU.add,
                )

        def new_parts(n):
            part_h[n] = blend_pool.tile([P, PACK, TILE_PIXELS], F32, tag="part_h", name="part_h")
            part_w[n] = blend_pool.tile([P, PACK, TILE_PIXELS], F32, tag="part_w", name="part_w")
            part_hc[n] = blend_pool.tile([P, PACK, TILE_PIXELS], F32, tag="part_hc", name="part_hc")

        def add_parts(engine, n, half, first, last):
            runs = slice(first // 4, last // 4)
            begin = half * HALF_PIXELS // 4
            source = slice(begin + first // 4, begin + last // 4)
            engine.tensor_tensor(
                out=fused[(n, half)][:].rearrange("p (c i t) -> p c t i", i=4, t=PACK)[:, runs, :, :],
                in0=part_hc[n][:].rearrange("p t (c i) -> p c t i", i=4)[:, source, :, :],
                in1=part_w[n][:].rearrange("p t (c i) -> p c t i", i=4)[:, source, :, :],
                op=ALU.add,
            )

        def output(n, s):
            image, half = divmod(n, SLOTS // TILE_SLOTS)
            codes, scales = fused_codes[(n, s // 2)]
            pixels = slice(s % 2 * P, (s % 2 + 1) * P)
            acc = psum.tile([P, C], F32, tag="bank", name="acc_out")
            nc.tensor.matmul_mx(
                out=acc[:],
                lhsT=codes[:, pixels].bitcast(FP8X4),
                lhsT_scale=scales[:, pixels],
                rhs=weights["p"][0][:].bitcast(FP8X4),
                rhs_scale=weights["p"][1][:],
                start=True,
                stop=True,
            )
            result = out_pool.tile([P, C], F32, tag="result", name="result")
            nc.vector.tensor_tensor(out=result[:], in0=acc[:], in1=bp_all[:], op=ALU.add)
            nc.sync.dma_start(
                out=out[image].rearrange("i (q s) e -> (i q) s e", s=SLOTS)[:, half * TILE_SLOTS + s, :],
                in_=result[:],
            )

        ident = consts.tile([P, P], F32, name="ident")
        make_identity(nc, ident[:])

        logits_bf = consts.tile([P, IMAGES, PACK * 3], BF16, name="logits_bf")
        nc.scalar.dma_start(out=logits_bf[:], in_=a_logits.rearrange("b (p c) -> p b c", c=PACK * 3))
        bias_h = consts.tile([P, PACK], BF16, name="bias_h")
        nc.scalar.dma_start(out=bias_h[:], in_=bo_h.rearrange("(p t) -> p t", t=PACK))
        bias_w = consts.tile([P, PACK], BF16, name="bias_w")
        nc.scalar.dma_start(out=bias_w[:], in_=bo_w.rearrange("(p t) -> p t", t=PACK))

        raw_tokens = {}
        raw_weights = {}
        branch_weights = {"h": Wo_h, "w": Wo_w, "c": Wmlpc}
        for branch in BRANCHES:
            raw_weights[branch] = load_weight(
                branch_weights[branch].rearrange("(p t) k -> p t k", t=PACK), branch
            )
            raw_tokens[(0, branch)] = load_tokens(0, branch)
        for branch in BRANCHES:
            raw_tokens[(1, branch)] = load_tokens(1, branch)
        raw_weights["p"] = load_weight(Wp.rearrange("(s p) d -> p s d", p=P), "p")
        bp_all = consts.tile([P, C], BF16, name="bp_all")
        nc.sync.dma_start(out=bp_all[:], in_=bp.partition_broadcast(P))
        for n in range(2, RAW_BUFS):
            for branch in BRANCHES:
                raw_tokens[(n, branch)] = load_tokens(n, branch)

        groups = IMAGES * PACK
        logits = consts.tile([P, groups, 3], F32, name="logits")
        top = consts.tile([P, groups], F32, name="top")
        expd = consts.tile([P, groups, 3], F32, name="expd")
        total = consts.tile([P, groups], F32, name="total")
        inverse = consts.tile([P, groups], F32, name="inverse")
        gate = consts.tile([P, groups, 3], F32, name="gate")
        by_image = gate[:].rearrange("p (b t) k -> p b t k", t=PACK)
        shift = consts.tile([P, groups], F32, name="shift")
        shift_w = consts.tile([P, groups], F32, name="shift_w")
        nc.vector.tensor_copy(out=logits[:], in_=logits_bf[:].rearrange("p b (t k) -> p (b t) k", k=3))
        nc.vector.tensor_reduce(out=top[:], in_=logits[:], axis=AXIS.X, op=ALU.max)
        nc.vector.tensor_tensor(
            out=logits[:], in0=logits[:], in1=top[:].unsqueeze(2).to_broadcast([P, groups, 3]), op=ALU.subtract
        )
        nc.scalar.activation(out=expd[:], in_=logits[:], func=ACT.Exp)

        def softmax_step(step):
            if step == 0:
                nc.vector.tensor_reduce(out=total[:], in_=expd[:], axis=AXIS.X, op=ALU.add)
            elif step == 1:
                nc.vector.reciprocal(out=inverse[:], in_=total[:])
            elif step == 2:
                nc.vector.tensor_tensor(
                    out=gate[:], in0=expd[:], in1=inverse[:].unsqueeze(2).to_broadcast([P, groups, 3]), op=ALU.mult
                )
            elif step == 3:
                nc.vector.tensor_tensor(
                    out=shift[:].rearrange("p (b t) -> p b t", t=PACK), in0=by_image[:, :, :, 0],
                    in1=bias_h[:].unsqueeze(1).to_broadcast([P, IMAGES, PACK]), op=ALU.mult,
                )
                nc.vector.tensor_tensor(
                    out=shift_w[:].rearrange("p (b t) -> p b t", t=PACK), in0=by_image[:, :, :, 1],
                    in1=bias_w[:].unsqueeze(1).to_broadcast([P, IMAGES, PACK]), op=ALU.mult,
                )
            elif step == 4:
                nc.vector.tensor_tensor(out=shift[:], in0=shift[:], in1=shift_w[:], op=ALU.add)

        weights = {}
        turned_tokens = {}
        token_codes = {}
        fused = {}
        fused_codes = {}
        part_h = {}
        part_w = {}
        part_hc = {}
        new_parts(0)
        turned_weights = {}
        def ready_branch(branch):
            turned_weights[branch] = turn(raw_weights[branch])
            if branch == "h":
                softmax_step(3)
            weights[branch] = quantise(turned_weights[branch], consts, "weight_" + branch)
            if branch == "h":
                softmax_step(4)
            turned_tokens[(0, branch)] = turn(raw_tokens[(0, branch)])
            raw_tokens[(RAW_BUFS, branch)] = load_tokens(RAW_BUFS, branch)
            quantise_tokens(0, branch)

        for step in range(3):
            softmax_step(step)
        for place, branch in enumerate(BRANCHES):
            turned_weights[branch] = turn(raw_weights[branch])
            if place > 0:
                quantise_tokens(0, BRANCHES[place - 1])
            else:
                softmax_step(3)
            turned_tokens[(0, branch)] = turn(raw_tokens[(0, branch)])
            raw_tokens[(RAW_BUFS, branch)] = load_tokens(RAW_BUFS, branch)
            weights[branch] = quantise(turned_weights[branch], consts, "weight_" + branch)
            if place == 0:
                softmax_step(4)
        quantise_tokens(0, "c")
        for branch in PROJECT_ORDER:
            for t in range(PACK):
                weigh(project(0, t, branch), 0, t, branch)
        for bank in range(6):
            turn_tokens_bank(1, bank, nc.vector.tensor_copy if bank % 2 == 1 else nc.scalar.copy)
            if bank in (3, 5):
                quantise_tokens(1, BRANCHES[bank // 2 - 1])
        turned_wp = turn(raw_weights["p"])
        quantise_tokens(1, "c")
        for bank in range(3):
            turn_tokens_bank(2, bank, nc.vector.tensor_copy if bank == 1 else nc.scalar.copy)
        weights["p"] = quantise(turned_wp, consts, "weight_p")

        for step in range(2, 2 * TILES + 4):
            n, half = divmod(step, 2)
            blend = n <= TILES
            gpsimd_pixels = GPSIMD_PIXELS if n < TILES else LAST_GPSIMD_PIXELS
            if blend:
                fused[(n - 1, half)] = blend_pool.tile(
                    [P, HALF_PIXELS * PACK], BF16, tag="fused", name="fused", align_bytes=64, bufs=1
                )
                add_parts(nc.gpsimd, n - 1, half, 0, gpsimd_pixels)
            if n < TILES and half == 0:
                new_parts(n)
            done = step - 4
            if done >= 0:
                for t in range(2):
                    output(done // 2, done % 2 * 2 + t)
            if n < TILES:
                for branch in PROJECT_ORDER:
                    for t in range(2):
                        weigh(project(n, 2 * half + t, branch), n, 2 * half + t, branch)
            ahead, ahead_half = divmod(step + 3, 2)
            for bank in range(3):
                on_vector = half == 0 and bank == 0
                turn_tokens_bank(
                    ahead, ahead_half * 3 + bank, nc.vector.tensor_copy if on_vector else nc.scalar.copy
                )
            if half == 1:
                quantise_tokens(n + 1, "w")
            if blend and gpsimd_pixels < HALF_PIXELS:
                add_parts(nc.vector, n - 1, half, gpsimd_pixels, HALF_PIXELS)
            quantise_tokens(n + 1, "h" if half == 0 else "c")
            if blend:
                fused_codes[(n - 1, half)] = quantise(fused[(n - 1, half)], blend_pool, "f", HALF_PIXELS)
